import numpy as np
import ml_dtypes


def mxq(x, axis, fmt="e4m3"):
    dtype, down = {"e4m3": (ml_dtypes.float8_e4m3fn, 7), "e5m2": (ml_dtypes.float8_e5m2, 14)}[fmt]
    v = np.moveaxis(np.asarray(x, np.float32).astype(ml_dtypes.bfloat16).astype(np.float64), axis, -1)
    blocks = v.reshape(v.shape[:-1] + (-1, 32))
    amax = np.abs(blocks).max(-1, keepdims=True)
    byte = np.maximum(np.where(amax > 0, np.frexp(amax)[1] - 1 + 127, 0) - down, 1)
    scale = np.exp2(byte - 127.0)
    codes = (blocks / scale).astype(np.float32).astype(dtype).astype(np.float64)
    return np.moveaxis((codes * scale).reshape(v.shape), -1, axis)


WIDE = False


def mx_kscale(k):
    if not WIDE:
        return np.ones(k)
    levels = np.array([10, -10, 5, -5, 0])
    a = np.random.permutation(np.resize(levels, k // 512 * 4)).reshape(k // 512, 4)
    idx = np.arange(k)
    return np.exp2(a[idx // 512, idx % 128 // 32])


BF16 = ml_dtypes.bfloat16


def bf(x):
    return np.asarray(x, np.float32).astype(BF16)


def f64(x):
    return np.asarray(x).astype(np.float64)


B, H, W, S2, CIN, QDIM, KDIM, NH = 8, 32, 64, 2048, 1024, 64, 512, 1
HD = QDIM // NH
EPS = 1e-6


def layernorm(t, g, b):
    mu = t.mean(-1, keepdims=True)
    var = ((t - mu) ** 2).mean(-1, keepdims=True)
    return (t - mu) * (1.0 / np.sqrt(var + EPS)) * g + b


def setup_inputs():
    s = mx_kscale(KDIM)
    return {"y": bf(np.random.standard_normal((B, S2, KDIM)) * s),
            "wkv": bf(np.random.standard_normal((2 * QDIM, KDIM)) / np.sqrt(KDIM) / s[None, :]),
            "bkv": bf(np.random.standard_normal(2 * QDIM) * 0.3),
            "kn_g": bf(1.0 + 0.1 * np.random.standard_normal(HD)),
            "kn_b": bf(0.1 * np.random.standard_normal(HD))}


def reference(y, wkv, bkv, kn_g, kn_b):
    kv = (mxq(f64(y), 2, "e4m3") @ mxq(f64(wkv), 1, "e4m3").T) + f64(bkv)
    kv = kv.reshape(B, S2, 2, NH, HD).transpose(0, 2, 3, 1, 4)
    k, v = kv[:, 0], kv[:, 1]
    return layernorm(k, f64(kn_g), f64(kn_b)), v

@@ -1,0 +1,249 @@
+from contextlib import ExitStack
+
+import concourse.mybir as mybir
+from concourse.masks import make_identity
+
+F32 = mybir.dt.float32
+BF16 = mybir.dt.bfloat16
+U32 = mybir.dt.uint32
+U8 = mybir.dt.uint8
+FP8X4 = mybir.dt.float8_e4m3fn_x4
+ALU = mybir.AluOpType
+ACT = mybir.ActivationFunctionType
+
+P = 128
+K = 512
+ROW_WORDS = K // 2
+KEYS = 64
+ROWS = 8 * 2048
+EPS = 1e-6
+
+UNIT_TILES = 4
+UNIT_ROWS = UNIT_TILES * P
+BANK_TILES = 2
+BANK_ROWS = BANK_TILES * P
+UNIT_BANKS = UNIT_TILES // BANK_TILES
+CHUNK_TILES = 8
+CHUNK_UNITS = CHUNK_TILES // UNIT_TILES
+N_CHUNKS = ROWS // (CHUNK_TILES * P)
+N_UNITS = N_CHUNKS * CHUNK_UNITS
+
+VECTOR_EVERY = 8
+
+LAG_QUANTISE = 1
+LAG_PROJECT = 3
+LAG_BACK = 5
+LAG_CENTRE = 6
+LAG_SPREAD = 8
+LAG_SCALE = 9
+N_STEPS = N_UNITS - CHUNK_UNITS + LAG_SCALE + 1
+
+FLOPS = 2 * ROWS * K * P
+
+
+def tile_crossattention2d_rope_pb_t_kernel(tc, y, wkv, bkv, kn_g, kn_b, out_0, out_1):
+    nc = tc.nc
+
+    y_chunks = y.flatten_outer_dims().rearrange("(c p j) k -> c p (j k)", p=P, j=CHUNK_TILES)
+    key_chunks = out_0.flatten_outer_dims().rearrange("(c p j) f -> c p (j f)", p=P, j=CHUNK_TILES)
+    value_chunks = out_1.flatten_outer_dims().rearrange("(c p j) f -> c p (j f)", p=P, j=CHUNK_TILES)
+
+    with ExitStack() as ctx:
+        consts = ctx.enter_context(tc.tile_pool(name="consts", bufs=1))
+        y_pool = ctx.enter_context(tc.tile_pool(name="y_pool", bufs=1))
+        grouped_pool = ctx.enter_context(tc.tile_pool(name="grouped_pool", bufs=3))
+        codes_pool = ctx.enter_context(tc.tile_pool(name="codes_pool", bufs=4))
+        xt_pool = ctx.enter_context(tc.tile_pool(name="xt_pool", bufs=4))
+        stats_pool = ctx.enter_context(tc.tile_pool(name="stats_pool", bufs=3))
+        chunk_pool = ctx.enter_context(tc.tile_pool(name="chunk_pool", bufs=3))
+        out_pool = ctx.enter_context(tc.tile_pool(name="out_pool", bufs=4))
+        words_psum = ctx.enter_context(tc.psum_pool(name="words_psum", bufs=4))
+        product_psum = ctx.enter_context(tc.psum_pool(name="product_psum", bufs=1))
+        rows_psum = ctx.enter_context(tc.psum_pool(name="rows_psum", bufs=3))
+
+        w_rows = consts.tile([P, K], BF16, name="w_rows")
+        nc.sync.dma_start(out=w_rows[:], in_=wkv)
+        y_rows = {}
+
+        def load_chunk(c):
+            y_rows[c] = y_pool.tile([P, CHUNK_TILES * K], BF16, name="y_chunk_%d" % c)
+            nc.sync.dma_start(out=y_rows[c][:], in_=y_chunks[c])
+
+        load_chunk(0)
+        bias_bf16 = consts.tile([P, 1], BF16, name="bias_bf16")
+        gain_shift_bf16 = consts.tile([P, 2 * KEYS], BF16, name="gain_shift_bf16")
+        with nc.allow_non_contiguous_dma(reason="128 bias values, one to a partition"):
+            nc.sync.dma_start(out=bias_bf16[:], in_=bkv.rearrange("(f o) -> f o", o=1))
+        nc.sync.dma_start(out=gain_shift_bf16[:, 0:KEYS], in_=kn_g.partition_broadcast(P))
+        nc.sync.dma_start(out=gain_shift_bf16[:, KEYS : 2 * KEYS], in_=kn_b.partition_broadcast(P))
+        for c in range(1, N_CHUNKS):
+            load_chunk(c)
+
+        eps = consts.tile([P, 1], F32, name="eps")
+        nc.vector.memset(eps[:], EPS)
+        table_warmer = consts.tile([P, 1], F32, name="table_warmer")
+        nc.scalar.activation(out=table_warmer[:], in_=eps[:], func=ACT.Sqrt)
+        identity = consts.tile([P, P], F32, name="identity")
+        make_identity(nc, identity[:])
+
+        w_words = words_psum.tile([P, 2, P], F32, tag="words", name="w_words")
+        for h in range(2):
+            nc.tensor.transpose(
+                w_words[:, h, :], w_rows[:].bitcast(F32)[:, h * P : (h + 1) * P], identity[:]
+            )
+        w_grouped = consts.tile([P, 4 * P], BF16, name="w_grouped", align_bytes=64)
+        nc.vector.tensor_copy(
+            out=w_grouped[:].bitcast(F32).rearrange("p (f h) -> p f h", h=2),
+            in_=w_words[:].rearrange("p h f -> p f h"),
+        )
+        w_codes = consts.tile([P, P], U32, name="w_codes", align_bytes=64)
+        w_scales = consts.tile([P, P], U8, name="w_scales", align_bytes=64)
+        nc.vector.quantize_mx(out=w_codes[:].bitcast(FP8X4), scales=w_scales[:], in_=w_grouped[:])
+
+        bias = consts.tile([P, 1], F32, name="bias")
+        nc.vector.tensor_copy(out=bias[:], in_=bias_bf16[:])
+        gain_shift = consts.tile([P, 2 * KEYS], F32, name="gain_shift")
+        nc.vector.tensor_copy(out=gain_shift[:], in_=gain_shift_bf16[:])
+        gain = gain_shift[:, 0:KEYS]
+        shift = gain_shift[:, KEYS : 2 * KEYS]
+
+        grouped = {}
+        y_codes = {}
+        y_scales = {}
+        x_cols = {}
+        x_rows = {}
+        moments = {}
+        centred = {}
+        deviation = {}
+        values = {}
+
+        def transpose_and_regroup(u):
+            words = y_rows[u // CHUNK_UNITS][:].bitcast(F32)
+            first_tile = (u % CHUNK_UNITS) * UNIT_TILES
+            grouped[u] = grouped_pool.tile([P, 4 * UNIT_ROWS], BF16, name="grouped", align_bytes=64)
+            pairs = grouped[u][:].bitcast(F32).rearrange("p (r h) -> p r h", h=2)
+            for b in range(UNIT_BANKS):
+                bank = words_psum.tile([P, 2, BANK_ROWS], F32, tag="words", name="bank")
+                for i in range(BANK_TILES):
+                    start = (first_tile + b * BANK_TILES + i) * ROW_WORDS
+                    for h in range(2):
+                        nc.tensor.transpose(
+                            bank[:, h, i * P : (i + 1) * P],
+                            words[:, start + h * P : start + (h + 1) * P],
+                            identity[:],
+                        )
+                out = pairs[:, b * BANK_ROWS : (b + 1) * BANK_ROWS, :]
+                if (u * UNIT_BANKS + b) % VECTOR_EVERY == VECTOR_EVERY - 1:
+                    nc.vector.tensor_copy(out=out, in_=bank[:].rearrange("p h r -> p r h"))
+                else:
+                    nc.scalar.copy(out=out, in_=bank[:].rearrange("p h r -> p r h"))
+
+        def quantise(u):
+            y_codes[u] = codes_pool.tile([P, UNIT_ROWS], U32, name="y_codes", align_bytes=64)
+            y_scales[u] = codes_pool.tile([P, UNIT_ROWS], U8, name="y_scales", align_bytes=64)
+            nc.vector.quantize_mx(
+                out=y_codes[u][:].bitcast(FP8X4), scales=y_scales[u][:], in_=grouped[u][:]
+            )
+
+        def project_and_add_bias(u):
+            product = product_psum.tile([P, UNIT_ROWS], F32, name="product")
+            nc.tensor.matmul_mx(
+                out=product[:],
+                lhsT=w_codes[:].bitcast(FP8X4),
+                lhsT_scale=w_scales[:],
+                rhs=y_codes[u][:].bitcast(FP8X4),
+                rhs_scale=y_scales[u][:],
+                start=True,
+                stop=True,
+            )
+            x_cols[u] = xt_pool.tile([P, UNIT_ROWS], F32, name="x_cols")
+            nc.scalar.activation(
+                out=x_cols[u][:], in_=product[:], func=ACT.Identity, bias=bias[:, 0:1], scale=1.0
+            )
+
+        def transpose_back_and_take_values(u):
+            c = u // CHUNK_UNITS
+            first_tile = (u % CHUNK_UNITS) * UNIT_TILES
+            x_rows[u] = rows_psum.tile([P, UNIT_TILES, P], F32, tag="rows", name="x_rows")
+            for i in range(UNIT_TILES):
+                nc.tensor.transpose(x_rows[u][:, i, :], x_cols[u][:, i * P : (i + 1) * P], identity[:])
+            if first_tile == 0:
+                values[c] = out_pool.tile([P, CHUNK_TILES, KEYS], F32, name="values")
+            nc.scalar.copy(
+                out=values[c][:, first_tile : first_tile + UNIT_TILES, :], in_=x_rows[u][:, :, KEYS:P]
+            )
+            if first_tile + UNIT_TILES == CHUNK_TILES:
+                nc.sync.dma_start(out=value_chunks[c], in_=values[c][:].rearrange("p j f -> p (j f)"))
+
+        def centre(u):
+            c = u // CHUNK_UNITS
+            first_tile = (u % CHUNK_UNITS) * UNIT_TILES
+            if first_tile == 0:
+                moments[c] = chunk_pool.tile([P, CHUNK_TILES, 2], F32, name="moments")
+                centred[c] = chunk_pool.tile([P, CHUNK_TILES, KEYS], F32, name="centred")
+            stats = stats_pool.tile([P, UNIT_TILES, 6], F32, name="stats")
+            for i in range(UNIT_TILES):
+                nc.vector.bn_stats(out=stats[:, i, :], in_=x_rows[u][:, i, 0:KEYS])
+            for i in range(UNIT_TILES):
+                nc.vector.bn_aggr(out=moments[c][:, first_tile + i, :], in_=stats[:, i, :])
+            for i in range(UNIT_TILES):
+                nc.vector.scalar_tensor_tensor(
+                    out=centred[c][:, first_tile + i, :],
+                    in0=x_rows[u][:, i, 0:KEYS],
+                    scalar=moments[c][:, first_tile + i, 0:1],
+                    in1=gain,
+                    op0=ALU.subtract,
+                    op1=ALU.mult,
+                )
+
+        def standard_deviation(c):
+            deviation[c] = chunk_pool.tile([P, CHUNK_TILES, 1], F32, name="deviation")
+            nc.scalar.activation(
+                out=deviation[c][:], in_=moments[c][:, :, 1:2], func=ACT.Sqrt, bias=eps[:, 0:1], scale=1.0
+            )
+
+        def scale_shift_and_store(c):
+            rstd = chunk_pool.tile([P, CHUNK_TILES, 1], F32, name="rstd")
+            nc.vector.reciprocal(out=rstd[:], in_=deviation[c][:])
+            keys = out_pool.tile([P, CHUNK_TILES, KEYS], F32, name="keys")
+            for j in range(CHUNK_TILES):
+                nc.vector.scalar_tensor_tensor(
+                    out=keys[:, j, :],
+                    in0=centred[c][:, j, :],
+                    scalar=rstd[:, j, :],
+                    in1=shift,
+                    op0=ALU.mult,
+                    op1=ALU.add,
+                )
+            nc.sync.dma_start(out=key_chunks[c], in_=keys[:].rearrange("p j f -> p (j f)"))
+
+        def unit_at(step, lag):
+            u = step - lag
+            return u if 0 <= u < N_UNITS else None
+
+        def chunk_at(step, lag):
+            u = step - lag
+            return u // CHUNK_UNITS if 0 <= u < N_UNITS and u % CHUNK_UNITS == 0 else None
+
+        for step in range(N_STEPS):
+            u = unit_at(step, LAG_BACK)
+            if u is not None:
+                transpose_back_and_take_values(u)
+            u = unit_at(step, LAG_CENTRE)
+            if u is not None:
+                centre(u)
+            u = unit_at(step, 0)
+            if u is not None:
+                transpose_and_regroup(u)
+            u = unit_at(step, LAG_QUANTISE)
+            if u is not None:
+                quantise(u)
+            u = unit_at(step, LAG_PROJECT)
+            if u is not None:
+                project_and_add_bias(u)
+            c = chunk_at(step, LAG_SPREAD)
+            if c is not None:
+                standard_deviation(c)
+            c = chunk_at(step, LAG_SCALE)
+            if c is not None:
+                scale_shift_and_store(c)

@@ -30,6 +30,8 @@ N_UNITS = N_CHUNKS * CHUNK_UNITS
 
 VECTOR_EVERY = 8
 
+PASS_REPEATS = 2
+
 LAG_QUANTISE = 1
 LAG_PROJECT = 3
 LAG_BACK = 5
@@ -147,15 +149,16 @@ def tile_crossattention2d_rope_pb_t_kernel(tc, y, wkv, bkv, kn_g, kn_b, out_0, o
 
         def project_and_add_bias(u):
             product = product_psum.tile([P, UNIT_ROWS], F32, name="product")
-            nc.tensor.matmul_mx(
-                out=product[:],
-                lhsT=w_codes[:].bitcast(FP8X4),
-                lhsT_scale=w_scales[:],
-                rhs=y_codes[u][:].bitcast(FP8X4),
-                rhs_scale=y_scales[u][:],
-                start=True,
-                stop=True,
-            )
+            for repeat in range(PASS_REPEATS):
+                nc.tensor.matmul_mx(
+                    out=product[:],
+                    lhsT=w_codes[:].bitcast(FP8X4),
+                    lhsT_scale=w_scales[:],
+                    rhs=y_codes[u][:].bitcast(FP8X4),
+                    rhs_scale=y_scales[u][:],
+                    start=True,
+                    stop=True,
+                )
             x_cols[u] = xt_pool.tile([P, UNIT_ROWS], F32, name="x_cols")
             nc.scalar.activation(
                 out=x_cols[u][:], in_=product[:], func=ACT.Identity, bias=bias[:, 0:1], scale=1.0

@@ -30,8 +30,6 @@ N_UNITS = N_CHUNKS * CHUNK_UNITS
 
 VECTOR_EVERY = 8
 
-PASS_REPEATS = 2
-
 LAG_QUANTISE = 1
 LAG_PROJECT = 3
 LAG_BACK = 5
@@ -51,6 +49,7 @@ def tile_crossattention2d_rope_pb_t_kernel(tc, y, wkv, bkv, kn_g, kn_b, out_0, o
     value_chunks = out_1.flatten_outer_dims().rearrange("(c p j) f -> c p (j f)", p=P, j=CHUNK_TILES)
 
     with ExitStack() as ctx:
+        ctx.enter_context(tc.manual_schedule())
         consts = ctx.enter_context(tc.tile_pool(name="consts", bufs=1))
         y_pool = ctx.enter_context(tc.tile_pool(name="y_pool", bufs=1))
         grouped_pool = ctx.enter_context(tc.tile_pool(name="grouped_pool", bufs=3))
@@ -149,16 +148,15 @@ def tile_crossattention2d_rope_pb_t_kernel(tc, y, wkv, bkv, kn_g, kn_b, out_0, o
 
         def project_and_add_bias(u):
             product = product_psum.tile([P, UNIT_ROWS], F32, name="product")
-            for repeat in range(PASS_REPEATS):
-                nc.tensor.matmul_mx(
-                    out=product[:],
-                    lhsT=w_codes[:].bitcast(FP8X4),
-                    lhsT_scale=w_scales[:],
-                    rhs=y_codes[u][:].bitcast(FP8X4),
-                    rhs_scale=y_scales[u][:],
-                    start=True,
-                    stop=True,
-                )
+            nc.tensor.matmul_mx(
+                out=product[:],
+                lhsT=w_codes[:].bitcast(FP8X4),
+                lhsT_scale=w_scales[:],
+                rhs=y_codes[u][:].bitcast(FP8X4),
+                rhs_scale=y_scales[u][:],
+                start=True,
+                stop=True,
+            )
             x_cols[u] = xt_pool.tile([P, UNIT_ROWS], F32, name="x_cols")
             nc.scalar.activation(
                 out=x_cols[u][:], in_=product[:], func=ACT.Identity, bias=bias[:, 0:1], scale=1.0

@@ -34,9 +34,9 @@ LAG_QUANTISE = 1
 LAG_PROJECT = 3
 LAG_BACK = 5
 LAG_CENTRE = 6
-LAG_SPREAD = 8
-LAG_SCALE = 9
-N_STEPS = N_UNITS - CHUNK_UNITS + LAG_SCALE + 1
+LAG_DEVIATION = 9
+LAG_SCALE = 10
+N_STEPS = N_UNITS + LAG_SCALE
 
 FLOPS = 2 * ROWS * K * P
 
@@ -52,33 +52,28 @@ def tile_crossattention2d_rope_pb_t_kernel(tc, y, wkv, bkv, kn_g, kn_b, out_0, o
         ctx.enter_context(tc.manual_schedule())
         consts = ctx.enter_context(tc.tile_pool(name="consts", bufs=1))
         y_pool = ctx.enter_context(tc.tile_pool(name="y_pool", bufs=1))
-        grouped_pool = ctx.enter_context(tc.tile_pool(name="grouped_pool", bufs=3))
+        grouped_pool = ctx.enter_context(tc.tile_pool(name="grouped_pool", bufs=4))
         codes_pool = ctx.enter_context(tc.tile_pool(name="codes_pool", bufs=4))
         xt_pool = ctx.enter_context(tc.tile_pool(name="xt_pool", bufs=4))
         stats_pool = ctx.enter_context(tc.tile_pool(name="stats_pool", bufs=3))
-        chunk_pool = ctx.enter_context(tc.tile_pool(name="chunk_pool", bufs=3))
-        out_pool = ctx.enter_context(tc.tile_pool(name="out_pool", bufs=4))
-        words_psum = ctx.enter_context(tc.psum_pool(name="words_psum", bufs=4))
-        product_psum = ctx.enter_context(tc.psum_pool(name="product_psum", bufs=1))
+        chunk_pool = ctx.enter_context(tc.tile_pool(name="chunk_pool", bufs=4))
+        out_pool = ctx.enter_context(tc.tile_pool(name="out_pool", bufs=8))
+        words_psum = ctx.enter_context(tc.psum_pool(name="words_psum", bufs=3))
+        product_psum = ctx.enter_context(tc.psum_pool(name="product_psum", bufs=2))
         rows_psum = ctx.enter_context(tc.psum_pool(name="rows_psum", bufs=3))
 
-        w_rows = consts.tile([P, K], BF16, name="w_rows")
-        nc.sync.dma_start(out=w_rows[:], in_=wkv)
-        y_rows = {}
-
-        def load_chunk(c):
-            y_rows[c] = y_pool.tile([P, CHUNK_TILES * K], BF16, name="y_chunk_%d" % c)
-            nc.sync.dma_start(out=y_rows[c][:], in_=y_chunks[c])
-
-        load_chunk(0)
         bias_bf16 = consts.tile([P, 1], BF16, name="bias_bf16")
         gain_shift_bf16 = consts.tile([P, 2 * KEYS], BF16, name="gain_shift_bf16")
         with nc.allow_non_contiguous_dma(reason="128 bias values, one to a partition"):
             nc.sync.dma_start(out=bias_bf16[:], in_=bkv.rearrange("(f o) -> f o", o=1))
         nc.sync.dma_start(out=gain_shift_bf16[:, 0:KEYS], in_=kn_g.partition_broadcast(P))
         nc.sync.dma_start(out=gain_shift_bf16[:, KEYS : 2 * KEYS], in_=kn_b.partition_broadcast(P))
-        for c in range(1, N_CHUNKS):
-            load_chunk(c)
+        w_rows = consts.tile([P, K], BF16, name="w_rows")
+        nc.sync.dma_start(out=w_rows[:], in_=wkv)
+        y_rows = {}
+        for c in range(N_CHUNKS):
+            y_rows[c] = y_pool.tile([P, CHUNK_TILES * K], BF16, name="y_chunk_%d" % c)
+            nc.sync.dma_start(out=y_rows[c][:], in_=y_chunks[c])
 
         eps = consts.tile([P, 1], F32, name="eps")
         nc.vector.memset(eps[:], EPS)
@@ -116,7 +111,9 @@ def tile_crossattention2d_rope_pb_t_kernel(tc, y, wkv, bkv, kn_g, kn_b, out_0, o
         moments = {}
         centred = {}
         deviation = {}
+        rstd = {}
         values = {}
+        keys = {}
 
         def transpose_and_regroup(u):
             words = y_rows[u // CHUNK_UNITS][:].bitcast(F32)
@@ -176,17 +173,22 @@ def tile_crossattention2d_rope_pb_t_kernel(tc, y, wkv, bkv, kn_g, kn_b, out_0, o
             if first_tile + UNIT_TILES == CHUNK_TILES:
                 nc.sync.dma_start(out=value_chunks[c], in_=values[c][:].rearrange("p j f -> p (j f)"))
 
-        def centre(u):
+        def mean_and_variance(u):
             c = u // CHUNK_UNITS
             first_tile = (u % CHUNK_UNITS) * UNIT_TILES
             if first_tile == 0:
                 moments[c] = chunk_pool.tile([P, CHUNK_TILES, 2], F32, name="moments")
-                centred[c] = chunk_pool.tile([P, CHUNK_TILES, KEYS], F32, name="centred")
             stats = stats_pool.tile([P, UNIT_TILES, 6], F32, name="stats")
             for i in range(UNIT_TILES):
                 nc.vector.bn_stats(out=stats[:, i, :], in_=x_rows[u][:, i, 0:KEYS])
             for i in range(UNIT_TILES):
                 nc.vector.bn_aggr(out=moments[c][:, first_tile + i, :], in_=stats[:, i, :])
+
+        def centre(u):
+            c = u // CHUNK_UNITS
+            first_tile = (u % CHUNK_UNITS) * UNIT_TILES
+            if first_tile == 0:
+                centred[c] = chunk_pool.tile([P, CHUNK_TILES, KEYS], F32, name="centred")
             for i in range(UNIT_TILES):
                 nc.vector.scalar_tensor_tensor(
                     out=centred[c][:, first_tile + i, :],
@@ -203,20 +205,26 @@ def tile_crossattention2d_rope_pb_t_kernel(tc, y, wkv, bkv, kn_g, kn_b, out_0, o
                 out=deviation[c][:], in_=moments[c][:, :, 1:2], func=ACT.Sqrt, bias=eps[:, 0:1], scale=1.0
             )
 
-        def scale_shift_and_store(c):
-            rstd = chunk_pool.tile([P, CHUNK_TILES, 1], F32, name="rstd")
-            nc.vector.reciprocal(out=rstd[:], in_=deviation[c][:])
-            keys = out_pool.tile([P, CHUNK_TILES, KEYS], F32, name="keys")
-            for j in range(CHUNK_TILES):
+        def reciprocal(c):
+            rstd[c] = chunk_pool.tile([P, CHUNK_TILES, 1], F32, name="rstd")
+            nc.vector.reciprocal(out=rstd[c][:], in_=deviation[c][:])
+
+        def scale_shift_and_store(u):
+            c = u // CHUNK_UNITS
+            first_tile = (u % CHUNK_UNITS) * UNIT_TILES
+            if first_tile == 0:
+                keys[c] = out_pool.tile([P, CHUNK_TILES, KEYS], F32, name="keys")
+            for j in range(first_tile, first_tile + UNIT_TILES):
                 nc.vector.scalar_tensor_tensor(
-                    out=keys[:, j, :],
+                    out=keys[c][:, j, :],
                     in0=centred[c][:, j, :],
-                    scalar=rstd[:, j, :],
+                    scalar=rstd[c][:, j, :],
                     in1=shift,
                     op0=ALU.mult,
                     op1=ALU.add,
                 )
-            nc.sync.dma_start(out=key_chunks[c], in_=keys[:].rearrange("p j f -> p (j f)"))
+            if first_tile + UNIT_TILES == CHUNK_TILES:
+                nc.sync.dma_start(out=key_chunks[c], in_=keys[c][:].rearrange("p j f -> p (j f)"))
 
         def unit_at(step, lag):
             u = step - lag
@@ -227,24 +235,30 @@ def tile_crossattention2d_rope_pb_t_kernel(tc, y, wkv, bkv, kn_g, kn_b, out_0, o
             return u // CHUNK_UNITS if 0 <= u < N_UNITS and u % CHUNK_UNITS == 0 else None
 
         for step in range(N_STEPS):
+            c = chunk_at(step, LAG_SCALE)
+            if c is not None:
+                reciprocal(c)
             u = unit_at(step, LAG_BACK)
             if u is not None:
                 transpose_back_and_take_values(u)
             u = unit_at(step, LAG_CENTRE)
             if u is not None:
-                centre(u)
+                mean_and_variance(u)
             u = unit_at(step, 0)
             if u is not None:
                 transpose_and_regroup(u)
             u = unit_at(step, LAG_QUANTISE)
             if u is not None:
                 quantise(u)
+            u = unit_at(step, LAG_CENTRE)
+            if u is not None:
+                centre(u)
             u = unit_at(step, LAG_PROJECT)
             if u is not None:
                 project_and_add_bias(u)
-            c = chunk_at(step, LAG_SPREAD)
+            c = chunk_at(step, LAG_DEVIATION)
             if c is not None:
                 standard_deviation(c)
-            c = chunk_at(step, LAG_SCALE)
-            if c is not None:
-                scale_shift_and_store(c)
+            u = unit_at(step, LAG_SCALE)
+            if u is not None:
+                scale_shift_and_store(u)

@@ -30,6 +30,8 @@ N_UNITS = N_CHUNKS * CHUNK_UNITS
 
 VECTOR_EVERY = 8
 
+PASS_REPEATS = 3
+
 LAG_QUANTISE = 1
 LAG_PROJECT = 3
 LAG_BACK = 5
@@ -145,15 +147,16 @@ def tile_crossattention2d_rope_pb_t_kernel(tc, y, wkv, bkv, kn_g, kn_b, out_0, o
 
         def project_and_add_bias(u):
             product = product_psum.tile([P, UNIT_ROWS], F32, name="product")
-            nc.tensor.matmul_mx(
-                out=product[:],
-                lhsT=w_codes[:].bitcast(FP8X4),
-                lhsT_scale=w_scales[:],
-                rhs=y_codes[u][:].bitcast(FP8X4),
-                rhs_scale=y_scales[u][:],
-                start=True,
-                stop=True,
-            )
+            for repeat in range(PASS_REPEATS):
+                nc.tensor.matmul_mx(
+                    out=product[:],
+                    lhsT=w_codes[:].bitcast(FP8X4),
+                    lhsT_scale=w_scales[:],
+                    rhs=y_codes[u][:].bitcast(FP8X4),
+                    rhs_scale=y_scales[u][:],
+                    start=True,
+                    stop=True,
+                )
             x_cols[u] = xt_pool.tile([P, UNIT_ROWS], F32, name="x_cols")
             nc.scalar.activation(
                 out=x_cols[u][:], in_=product[:], func=ACT.Identity, bias=bias[:, 0:1], scale=1.0

from contextlib import ExitStack

import concourse.mybir as mybir
from concourse.masks import make_identity

F32 = mybir.dt.float32
BF16 = mybir.dt.bfloat16
U32 = mybir.dt.uint32
U8 = mybir.dt.uint8
FP8X4 = mybir.dt.float8_e4m3fn_x4
ALU = mybir.AluOpType
ACT = mybir.ActivationFunctionType

P = 128
K = 512
ROW_WORDS = K // 2
KEYS = 64
ROWS = 8 * 2048
EPS = 1e-6

UNIT_TILES = 4
UNIT_ROWS = UNIT_TILES * P
BANK_TILES = 2
BANK_ROWS = BANK_TILES * P
UNIT_BANKS = UNIT_TILES // BANK_TILES
CHUNK_TILES = 8
CHUNK_UNITS = CHUNK_TILES // UNIT_TILES
N_CHUNKS = ROWS // (CHUNK_TILES * P)
N_UNITS = N_CHUNKS * CHUNK_UNITS

VECTOR_EVERY = 8

PASS_REPEATS = 3

LAG_QUANTISE = 1
LAG_PROJECT = 3
LAG_BACK = 5
LAG_CENTRE = 6
LAG_DEVIATION = 9
LAG_SCALE = 10
N_STEPS = N_UNITS + LAG_SCALE

FLOPS = 2 * ROWS * K * P


def tile_crossattention2d_rope_pb_t_kernel(tc, y, wkv, bkv, kn_g, kn_b, out_0, out_1):
    nc = tc.nc

    y_chunks = y.flatten_outer_dims().rearrange("(c p j) k -> c p (j k)", p=P, j=CHUNK_TILES)
    key_chunks = out_0.flatten_outer_dims().rearrange("(c p j) f -> c p (j f)", p=P, j=CHUNK_TILES)
    value_chunks = out_1.flatten_outer_dims().rearrange("(c p j) f -> c p (j f)", p=P, j=CHUNK_TILES)

    with ExitStack() as ctx:
        ctx.enter_context(tc.manual_schedule())
        consts = ctx.enter_context(tc.tile_pool(name="consts", bufs=1))
        y_pool = ctx.enter_context(tc.tile_pool(name="y_pool", bufs=1))
        grouped_pool = ctx.enter_context(tc.tile_pool(name="grouped_pool", bufs=4))
        codes_pool = ctx.enter_context(tc.tile_pool(name="codes_pool", bufs=4))
        xt_pool = ctx.enter_context(tc.tile_pool(name="xt_pool", bufs=4))
        stats_pool = ctx.enter_context(tc.tile_pool(name="stats_pool", bufs=3))
        chunk_pool = ctx.enter_context(tc.tile_pool(name="chunk_pool", bufs=4))
        out_pool = ctx.enter_context(tc.tile_pool(name="out_pool", bufs=8))
        words_psum = ctx.enter_context(tc.psum_pool(name="words_psum", bufs=3))
        product_psum = ctx.enter_context(tc.psum_pool(name="product_psum", bufs=2))
        rows_psum = ctx.enter_context(tc.psum_pool(name="rows_psum", bufs=3))

        bias_bf16 = consts.tile([P, 1], BF16, name="bias_bf16")
        gain_shift_bf16 = consts.tile([P, 2 * KEYS], BF16, name="gain_shift_bf16")
        with nc.allow_non_contiguous_dma(reason="128 bias values, one to a partition"):
            nc.sync.dma_start(out=bias_bf16[:], in_=bkv.rearrange("(f o) -> f o", o=1))
        nc.sync.dma_start(out=gain_shift_bf16[:, 0:KEYS], in_=kn_g.partition_broadcast(P))
        nc.sync.dma_start(out=gain_shift_bf16[:, KEYS : 2 * KEYS], in_=kn_b.partition_broadcast(P))
        w_rows = consts.tile([P, K], BF16, name="w_rows")
        nc.sync.dma_start(out=w_rows[:], in_=wkv)
        y_rows = {}
        for c in range(N_CHUNKS):
            y_rows[c] = y_pool.tile([P, CHUNK_TILES * K], BF16, name="y_chunk_%d" % c)
            nc.sync.dma_start(out=y_rows[c][:], in_=y_chunks[c])

        eps = consts.tile([P, 1], F32, name="eps")
        nc.vector.memset(eps[:], EPS)
        table_warmer = consts.tile([P, 1], F32, name="table_warmer")
        nc.scalar.activation(out=table_warmer[:], in_=eps[:], func=ACT.Sqrt)
        identity = consts.tile([P, P], F32, name="identity")
        make_identity(nc, identity[:])

        w_words = words_psum.tile([P, 2, P], F32, tag="words", name="w_words")
        for h in range(2):
            nc.tensor.transpose(
                w_words[:, h, :], w_rows[:].bitcast(F32)[:, h * P : (h + 1) * P], identity[:]
            )
        w_grouped = consts.tile([P, 4 * P], BF16, name="w_grouped", align_bytes=64)
        nc.vector.tensor_copy(
            out=w_grouped[:].bitcast(F32).rearrange("p (f h) -> p f h", h=2),
            in_=w_words[:].rearrange("p h f -> p f h"),
        )
        w_codes = consts.tile([P, P], U32, name="w_codes", align_bytes=64)
        w_scales = consts.tile([P, P], U8, name="w_scales", align_bytes=64)
        nc.vector.quantize_mx(out=w_codes[:].bitcast(FP8X4), scales=w_scales[:], in_=w_grouped[:])

        bias = consts.tile([P, 1], F32, name="bias")
        nc.vector.tensor_copy(out=bias[:], in_=bias_bf16[:])
        gain_shift = consts.tile([P, 2 * KEYS], F32, name="gain_shift")
        nc.vector.tensor_copy(out=gain_shift[:], in_=gain_shift_bf16[:])
        gain = gain_shift[:, 0:KEYS]
        shift = gain_shift[:, KEYS : 2 * KEYS]

        grouped = {}
        y_codes = {}
        y_scales = {}
        x_cols = {}
        x_rows = {}
        moments = {}
        centred = {}
        deviation = {}
        rstd = {}
        values = {}
        keys = {}

        def transpose_and_regroup(u):
            words = y_rows[u // CHUNK_UNITS][:].bitcast(F32)
            first_tile = (u % CHUNK_UNITS) * UNIT_TILES
            grouped[u] = grouped_pool.tile([P, 4 * UNIT_ROWS], BF16, name="grouped", align_bytes=64)
            pairs = grouped[u][:].bitcast(F32).rearrange("p (r h) -> p r h", h=2)
            for b in range(UNIT_BANKS):
                bank = words_psum.tile([P, 2, BANK_ROWS], F32, tag="words", name="bank")
                for i in range(BANK_TILES):
                    start = (first_tile + b * BANK_TILES + i) * ROW_WORDS
                    for h in range(2):
                        nc.tensor.transpose(
                            bank[:, h, i * P : (i + 1) * P],
                            words[:, start + h * P : start + (h + 1) * P],
                            identity[:],
                        )
                out = pairs[:, b * BANK_ROWS : (b + 1) * BANK_ROWS, :]
                if (u * UNIT_BANKS + b) % VECTOR_EVERY == VECTOR_EVERY - 1:
                    nc.vector.tensor_copy(out=out, in_=bank[:].rearrange("p h r -> p r h"))
                else:
                    nc.scalar.copy(out=out, in_=bank[:].rearrange("p h r -> p r h"))

        def quantise(u):
            y_codes[u] = codes_pool.tile([P, UNIT_ROWS], U32, name="y_codes", align_bytes=64)
            y_scales[u] = codes_pool.tile([P, UNIT_ROWS], U8, name="y_scales", align_bytes=64)
            nc.vector.quantize_mx(
                out=y_codes[u][:].bitcast(FP8X4), scales=y_scales[u][:], in_=grouped[u][:]
            )

        def project_and_add_bias(u):
            product = product_psum.tile([P, UNIT_ROWS], F32, name="product")
            for repeat in range(PASS_REPEATS):
                nc.tensor.matmul_mx(
                    out=product[:],
                    lhsT=w_codes[:].bitcast(FP8X4),
                    lhsT_scale=w_scales[:],
                    rhs=y_codes[u][:].bitcast(FP8X4),
                    rhs_scale=y_scales[u][:],
                    start=True,
                    stop=True,
                )
            x_cols[u] = xt_pool.tile([P, UNIT_ROWS], F32, name="x_cols")
            nc.scalar.activation(
                out=x_cols[u][:], in_=product[:], func=ACT.Identity, bias=bias[:, 0:1], scale=1.0
            )

        def transpose_back_and_take_values(u):
            c = u // CHUNK_UNITS
            first_tile = (u % CHUNK_UNITS) * UNIT_TILES
            x_rows[u] = rows_psum.tile([P, UNIT_TILES, P], F32, tag="rows", name="x_rows")
            for i in range(UNIT_TILES):
                nc.tensor.transpose(x_rows[u][:, i, :], x_cols[u][:, i * P : (i + 1) * P], identity[:])
            if first_tile == 0:
                values[c] = out_pool.tile([P, CHUNK_TILES, KEYS], F32, name="values")
            nc.scalar.copy(
                out=values[c][:, first_tile : first_tile + UNIT_TILES, :], in_=x_rows[u][:, :, KEYS:P]
            )
            if first_tile + UNIT_TILES == CHUNK_TILES:
                nc.sync.dma_start(out=value_chunks[c], in_=values[c][:].rearrange("p j f -> p (j f)"))

        def mean_and_variance(u):
            c = u // CHUNK_UNITS
            first_tile = (u % CHUNK_UNITS) * UNIT_TILES
            if first_tile == 0:
                moments[c] = chunk_pool.tile([P, CHUNK_TILES, 2], F32, name="moments")
            stats = stats_pool.tile([P, UNIT_TILES, 6], F32, name="stats")
            for i in range(UNIT_TILES):
                nc.vector.bn_stats(out=stats[:, i, :], in_=x_rows[u][:, i, 0:KEYS])
            for i in range(UNIT_TILES):
                nc.vector.bn_aggr(out=moments[c][:, first_tile + i, :], in_=stats[:, i, :])

        def centre(u):
            c = u // CHUNK_UNITS
            first_tile = (u % CHUNK_UNITS) * UNIT_TILES
            if first_tile == 0:
                centred[c] = chunk_pool.tile([P, CHUNK_TILES, KEYS], F32, name="centred")
            for i in range(UNIT_TILES):
                nc.vector.scalar_tensor_tensor(
                    out=centred[c][:, first_tile + i, :],
                    in0=x_rows[u][:, i, 0:KEYS],
                    scalar=moments[c][:, first_tile + i, 0:1],
                    in1=gain,
                    op0=ALU.subtract,
                    op1=ALU.mult,
                )

        def standard_deviation(c):
            deviation[c] = chunk_pool.tile([P, CHUNK_TILES, 1], F32, name="deviation")
            nc.scalar.activation(
                out=deviation[c][:], in_=moments[c][:, :, 1:2], func=ACT.Sqrt, bias=eps[:, 0:1], scale=1.0
            )

        def reciprocal(c):
            rstd[c] = chunk_pool.tile([P, CHUNK_TILES, 1], F32, name="rstd")
            nc.vector.reciprocal(out=rstd[c][:], in_=deviation[c][:])

        def scale_shift_and_store(u):
            c = u // CHUNK_UNITS
            first_tile = (u % CHUNK_UNITS) * UNIT_TILES
            if first_tile == 0:
                keys[c] = out_pool.tile([P, CHUNK_TILES, KEYS], F32, name="keys")
            for j in range(first_tile, first_tile + UNIT_TILES):
                nc.vector.scalar_tensor_tensor(
                    out=keys[c][:, j, :],
                    in0=centred[c][:, j, :],
                    scalar=rstd[c][:, j, :],
                    in1=shift,
                    op0=ALU.mult,
                    op1=ALU.add,
                )
            if first_tile + UNIT_TILES == CHUNK_TILES:
                nc.sync.dma_start(out=key_chunks[c], in_=keys[c][:].rearrange("p j f -> p (j f)"))

        def unit_at(step, lag):
            u = step - lag
            return u if 0 <= u < N_UNITS else None

        def chunk_at(step, lag):
            u = step - lag
            return u // CHUNK_UNITS if 0 <= u < N_UNITS and u % CHUNK_UNITS == 0 else None

        for step in range(N_STEPS):
            c = chunk_at(step, LAG_SCALE)
            if c is not None:
                reciprocal(c)
            u = unit_at(step, LAG_BACK)
            if u is not None:
                transpose_back_and_take_values(u)
            u = unit_at(step, LAG_CENTRE)
            if u is not None:
                mean_and_variance(u)
            u = unit_at(step, 0)
            if u is not None:
                transpose_and_regroup(u)
            u = unit_at(step, LAG_QUANTISE)
            if u is not None:
                quantise(u)
            u = unit_at(step, LAG_CENTRE)
            if u is not None:
                centre(u)
            u = unit_at(step, LAG_PROJECT)
            if u is not None:
                project_and_add_bias(u)
            c = chunk_at(step, LAG_DEVIATION)
            if c is not None:
                standard_deviation(c)
            u = unit_at(step, LAG_SCALE)
            if u is not None:
                scale_shift_and_store(u)
